import numpy as np
import ml_dtypes


def mxq(x, axis, fmt="e4m3"):
    dtype, down = {"e4m3": (ml_dtypes.float8_e4m3fn, 7), "e5m2": (ml_dtypes.float8_e5m2, 14)}[fmt]
    v = np.moveaxis(np.asarray(x, np.float32).astype(ml_dtypes.bfloat16).astype(np.float64), axis, -1)
    blocks = v.reshape(v.shape[:-1] + (-1, 32))
    amax = np.abs(blocks).max(-1, keepdims=True)
    byte = np.maximum(np.where(amax > 0, np.frexp(amax)[1] - 1 + 127, 0) - down, 1)
    scale = np.exp2(byte - 127.0)
    codes = (blocks / scale).astype(np.float32).astype(dtype).astype(np.float64)
    return np.moveaxis((codes * scale).reshape(v.shape), -1, axis)


WIDE = False


def mx_kscale(k):
    if not WIDE:
        return np.ones(k)
    levels = np.array([10, -10, 5, -5, 0])
    a = np.random.permutation(np.resize(levels, k // 512 * 4)).reshape(k // 512, 4)
    idx = np.arange(k)
    return np.exp2(a[idx // 512, idx % 128 // 32])


BF16 = ml_dtypes.bfloat16


def bf(x):
    return np.asarray(x, np.float32).astype(BF16)


def f64(x):
    return np.asarray(x).astype(np.float64)


E2M1 = np.array([0.0, 0.5, 1.0, 1.5, 2.0, 3.0, 4.0, 6.0, -0.0, -0.5, -1.0, -1.5, -2.0, -3.0, -4.0, -6.0])


def pack_weight(w, fmt):
    k, n = w.shape
    w = f64(bf(w)).reshape(k // 32, 32, n)
    amax = np.abs(w).max(1)
    if fmt == "e4m3":
        byte = np.frexp(amax)[1] - 1 + 127 - 7
    else:
        mant, ex = np.frexp(amax / 6.0)
        byte = np.where(mant > 0.5, ex, ex - 1) + 127
    byte = np.clip(np.where(amax > 0, byte, 1), 1, 254)
    scaled = (w * np.exp2(127.0 - byte)[:, None, :]).reshape(k, n).astype(np.float32)
    by_word = np.ascontiguousarray(scaled.reshape(k // 512, 128, 4, n).transpose(0, 1, 3, 2))
    if fmt == "e4m3":
        words = by_word.astype(ml_dtypes.float8_e4m3fn).view(np.uint8)
    else:
        c = by_word.astype(ml_dtypes.float4_e2m1fn).view(np.uint8) & 0xF
        words = c[..., 0::2] | (c[..., 1::2] << 4)
    return np.ascontiguousarray(words), np.ascontiguousarray(byte.astype(np.uint8).reshape(k // 512, 16, n))


def unpack_weight(words, scales, fmt):
    g, p, n, _ = words.shape
    if fmt == "e4m3":
        vals = np.ascontiguousarray(words).view(ml_dtypes.float8_e4m3fn).astype(np.float64)
    else:
        nib = np.empty((g, p, n, 4), np.uint8)
        nib[..., 0::2] = words & 0xF
        nib[..., 1::2] = words >> 4
        vals = E2M1[nib]
    vals = vals * np.repeat(np.exp2(scales.astype(np.float64) - 127.0), 8, axis=1)[..., None]
    return vals.transpose(0, 1, 3, 2).reshape(g * 512, n)

def pack4(w):
    words, scales = pack_weight(w, "e2m1")
    return words.reshape(words.shape[0], 128, -1), scales


def unpack4(words, scales):
    return unpack_weight(words.reshape(words.shape[0], 128, -1, 2), scales, "e2m1")


B, CIN, COUT, T, R, C = 2, 512, 512, 8, 8, 8


def setup_inputs():
    s = mx_kscale(CIN)
    x = np.random.standard_normal((B, CIN, T, R, C)) * s[None, :, None, None, None]
    W = np.random.standard_normal((7 * COUT, CIN)) * 0.5 / np.sqrt(CIN) / s[None, :]
    words, scales = pack4(np.ascontiguousarray(W.T))
    return {"x": bf(x), "W_words": words, "W_scales": scales}


def _shift(a, axis, d):
    pads = [(0, 0)] * a.ndim
    idx = [slice(None)] * a.ndim
    if d > 0:
        pads[axis] = (1, 0)
        idx[axis] = slice(0, -1)
    else:
        pads[axis] = (0, 1)
        idx[axis] = slice(1, None)
    return np.pad(a, pads)[tuple(idx)]


def reference(x, W_words, W_scales):
    cout = W_scales.shape[2] // 7
    xq = mxq(f64(x), 1, "e4m3")
    Wq = unpack4(W_words, W_scales).T
    all_out = xq.transpose(0, 2, 3, 4, 1) @ Wq.T
    a = all_out.reshape(*all_out.shape[:4], 7, cout)
    out = a[..., 0, :]
    out = out + _shift(a[..., 1, :], 1, +1)
    out = out + _shift(a[..., 2, :], 1, -1)
    out = out + _shift(a[..., 3, :], 2, +1)
    out = out + _shift(a[..., 4, :], 2, -1)
    out = out + _shift(a[..., 5, :], 3, +1)
    out = out + _shift(a[..., 6, :], 3, -1)
    return np.transpose(out, (0, 4, 1, 2, 3))

@@ -1,0 +1,154 @@
+from contextlib import ExitStack
+
+import concourse.mybir as mybir
+
+BF16 = mybir.dt.bfloat16
+F32 = mybir.dt.float32
+I32 = mybir.dt.int32
+U32 = mybir.dt.uint32
+U8 = mybir.dt.uint8
+FP8X4 = mybir.dt.float8_e4m3fn_x4
+FP4X4 = mybir.dt.float4_e2m1fn_x4
+
+P = 128
+B = 2
+V = 512
+OT = 4
+PAD = 64
+FLOPS = 2 * B * V * 512 * 7 * 512
+
+V_FIRST = 256
+V_SPLIT = 336
+
+
+def tile_stackeddirectionalconv3d_kernel(tc, x, W_words, W_scales, out):
+    nc = tc.nc
+    with ExitStack() as ctx:
+        keep = ctx.enter_context(tc.tile_pool(name="keep", bufs=1))
+        psum = ctx.enter_context(tc.psum_pool(name="psum", bufs=1))
+        ctx.enter_context(tc.manual_schedule())
+
+        raw = keep.tile([P, B, 4, V], BF16)
+        grouped = keep.tile([P, B, V, 4], BF16, align_bytes=64)
+        base_codes = keep.tile([P, B, V + 2 * PAD], U32, align_bytes=64)
+        base_scales = keep.tile([P, B, V + 2 * PAD], U8, align_bytes=64)
+        row_codes = keep.tile([P, 2, B, V], U32, align_bytes=64)
+        row_scales = keep.tile([P, 2, B, V], U8, align_bytes=64)
+        col_vals = keep.tile([P, 2, B, V, 4], BF16, align_bytes=64)
+        col_codes = keep.tile([P, 2, B, V], U32, align_bytes=64)
+        col_scales = keep.tile([P, 2, B, V], U8, align_bytes=64)
+        w_words = keep.tile([P, 7 * 1024], U8, align_bytes=64)
+        w_plane = keep.tile([P, 7 * 512], U8, align_bytes=64)
+        stage = keep.tile([P, B * OT, V], F32)
+        acc = [psum.tile([P, V], F32, name="acc%d" % k) for k in range(B * OT)]
+
+        x_view = x.rearrange("b (p j) t r c -> b p j (t r c)", j=4)
+        out_view = out.rearrange("b (o p) t r c -> b o p (t r c)", p=P)
+        w_dram = W_words[0].bitcast(I32)
+        w_sbuf = w_words[:].bitcast(I32)
+        split = 3 * 256
+
+        nc.sync.dma_start(out=raw[:, 0], in_=x_view[0])
+        nc.sync.dma_start(out=w_sbuf[:, 0:split], in_=w_dram[:, 0:split])
+        nc.vector.memset(w_plane[:].bitcast(I32), 0)
+        for q in range(4):
+            nc.sync.dma_start(
+                out=w_plane[32 * q : 32 * q + 4, :].bitcast(I32),
+                in_=W_scales[0, 4 * q : 4 * q + 4, :].bitcast(I32),
+            )
+        nc.sync.dma_start(out=raw[:, 1], in_=x_view[1])
+        nc.sync.dma_start(out=w_sbuf[:, split:], in_=w_dram[:, split:])
+
+        nc.vector.memset(
+            base_codes[:].bitcast(I32).rearrange("p b (a w) -> p b a w", w=PAD)[:, :, 0:10:9, :], 0
+        )
+        nc.vector.memset(base_scales[:].bitcast(I32), 0)
+        for i in range(2):
+            rc = row_codes[:, i].bitcast(I32).rearrange("p b (t w) -> p (b t) w", w=64)
+            rs = row_scales[:, i].bitcast(I32).rearrange("p b (t w) -> p (b t) w", w=16)
+            cv = col_vals[:, i].rearrange("p b (s c) j -> p (b s) (c j)", c=8)
+            if i == 0:
+                nc.vector.memset(rc[:, :, 0:8], 0)
+                nc.vector.memset(rs[:, :, 0:2], 0)
+                nc.vector.memset(cv[:, :, 0:4], 0.0)
+            else:
+                nc.vector.memset(rc[:, :, 56:64], 0)
+                nc.vector.memset(rs[:, :, 14:16], 0)
+                nc.vector.memset(cv[:, :, 28:32], 0.0)
+
+        def regroup(copy, b, v0, v1):
+            copy(
+                out=grouped[:, b, v0:v1, :].rearrange("p (c i) j -> p c j i", i=4),
+                in_=raw[:, b, :, v0:v1].rearrange("p j (c i) -> p c j i", i=4),
+            )
+
+        def quantise_base(b):
+            regroup(nc.vector.tensor_copy, b, 0, V_FIRST)
+            regroup(nc.scalar.copy, b, V_SPLIT, V)
+            regroup(nc.vector.tensor_copy, b, V_FIRST, V_SPLIT)
+            for h in range(2):
+                lo = 256 * h
+                nc.vector.quantize_mx(
+                    out=base_codes[:, b, PAD + lo : PAD + lo + 256].bitcast(FP8X4),
+                    scales=base_scales[:, b, PAD + lo : PAD + lo + 256],
+                    in_=grouped[:, b, lo : lo + 256, :].rearrange("p v j -> p (v j)"),
+                )
+
+        def shifted(b):
+            sc = base_codes[:, b, PAD : PAD + V].bitcast(I32).rearrange("p (t w) -> p t w", w=64)
+            ss = base_scales[:, b, PAD : PAD + V].bitcast(I32).rearrange("p (t w) -> p t w", w=16)
+            g = grouped[:, b].rearrange("p (s c) j -> p s (c j)", c=8)
+            dc = [row_codes[:, i, b, :].bitcast(I32).rearrange("p (t w) -> p t w", w=64) for i in range(2)]
+            ds = [row_scales[:, i, b, :].bitcast(I32).rearrange("p (t w) -> p t w", w=16) for i in range(2)]
+            dv = [col_vals[:, i, b].rearrange("p (s c) j -> p s (c j)", c=8) for i in range(2)]
+            nc.vector.tensor_copy(out=dc[0][:, :, 8:64], in_=sc[:, :, 0:56])
+            nc.vector.tensor_copy(out=ds[0][:, :, 2:16], in_=ss[:, :, 0:14])
+            nc.vector.tensor_copy(out=dc[1][:, :, 0:56], in_=sc[:, :, 8:64])
+            nc.vector.tensor_copy(out=ds[1][:, :, 0:14], in_=ss[:, :, 2:16])
+            nc.vector.tensor_copy(out=dv[0][:, :, 4:32], in_=g[:, :, 0:28])
+            nc.vector.tensor_copy(out=dv[1][:, :, 0:28], in_=g[:, :, 4:32])
+            for i in range(2):
+                nc.vector.quantize_mx(
+                    out=col_codes[:, i, b, :].bitcast(FP8X4),
+                    scales=col_scales[:, i, b, :],
+                    in_=col_vals[:, i, b].rearrange("p v j -> p (v j)"),
+                )
+
+        def moving(b, d):
+            if d < 3:
+                lo = (PAD, 0, 2 * PAD)[d]
+                return base_codes[:, b, lo : lo + V], base_scales[:, b, lo : lo + V]
+            if d < 5:
+                return row_codes[:, d - 3, b, :], row_scales[:, d - 3, b, :]
+            return col_codes[:, d - 5, b, :], col_scales[:, d - 5, b, :]
+
+        def mx_pass(b, o, d):
+            n = OT * d + o
+            codes, scales = moving(b, d)
+            nc.tensor.matmul_mx(
+                out=acc[OT * b + o][:],
+                lhsT=w_words[:, 256 * n : 256 * (n + 1)].bitcast(FP4X4),
+                lhsT_scale=w_plane[:, P * n : P * (n + 1)],
+                rhs=codes.bitcast(FP8X4),
+                rhs_scale=scales,
+                start=(d == 0),
+                stop=(d == 6),
+            )
+
+        for b in range(B):
+            quantise_base(b)
+            for d in range(3):
+                for o in range(OT):
+                    mx_pass(b, o, d)
+        for b in range(B):
+            shifted(b)
+        for b in range(B):
+            for o in range(OT):
+                for d in range(3, 7):
+                    mx_pass(b, o, d)
+                k = OT * b + o
+                if k % 2 == 0:
+                    nc.scalar.copy(out=stage[:, k, :], in_=acc[k][:])
+                else:
+                    nc.vector.tensor_copy(out=stage[:, k, :], in_=acc[k][:])
+                nc.sync.dma_start(out=out_view[b, o], in_=stage[:, k, :])

@@ -19,6 +19,8 @@ FLOPS = 2 * B * V * 512 * 7 * 512
 
 V_FIRST = 256
 V_SPLIT = 336
+WARM_EARLY = 5
+WARM_LATE = 3
 
 
 def tile_stackeddirectionalconv3d_kernel(tc, x, W_words, W_scales, out):
@@ -49,6 +51,12 @@ def tile_stackeddirectionalconv3d_kernel(tc, x, W_words, W_scales, out):
         split = 3 * 256
 
         nc.sync.dma_start(out=raw[:, 0], in_=x_view[0])
+        warm = keep.tile([P, V], BF16)
+        nc.vector.memset(warm[:], 0.0)
+        for i in range(WARM_EARLY):
+            nc.tensor.matmul(out=acc[7][:], lhsT=warm[:, 0:P], rhs=warm[:], start=True, stop=True)
+        for i in range(WARM_LATE):
+            nc.tensor.matmul(out=acc[7][:], lhsT=raw[:, 0, 0, 0:P], rhs=raw[:, 0, 1, :], start=True, stop=True)
         nc.sync.dma_start(out=w_sbuf[:, 0:split], in_=w_dram[:, 0:split])
         nc.vector.memset(w_plane[:].bitcast(I32), 0)
         for q in range(4):

@@ -42,7 +42,8 @@ def tile_stackeddirectionalconv3d_kernel(tc, x, W_words, W_scales, out):
         w_words = keep.tile([P, 7 * 1024], U8, align_bytes=64)
         w_plane = keep.tile([P, 7 * 512], U8, align_bytes=64)
         stage = keep.tile([P, B * OT, V], F32)
-        acc = [psum.tile([P, V], F32, name="acc%d" % k) for k in range(B * OT)]
+        acc = [psum.tile([P, V], F32, name="acc%d" % k) for k in range(B * OT - 1)]
+        warm_acc = psum.tile([P, V], F32)
 
         x_view = x.rearrange("b (p j) t r c -> b p j (t r c)", j=4)
         out_view = out.rearrange("b (o p) t r c -> b o p (t r c)", p=P)
@@ -54,9 +55,9 @@ def tile_stackeddirectionalconv3d_kernel(tc, x, W_words, W_scales, out):
         warm = keep.tile([P, V], BF16)
         nc.vector.memset(warm[:], 0.0)
         for i in range(WARM_EARLY):
-            nc.tensor.matmul(out=acc[7][:], lhsT=warm[:, 0:P], rhs=warm[:], start=True, stop=True)
+            nc.tensor.matmul(out=warm_acc[:], lhsT=warm[:, 0:P], rhs=warm[:], start=True, stop=True)
         for i in range(WARM_LATE):
-            nc.tensor.matmul(out=acc[7][:], lhsT=raw[:, 0, 0, 0:P], rhs=raw[:, 0, 1, :], start=True, stop=True)
+            nc.tensor.matmul(out=warm_acc[:], lhsT=raw[:, 0, 0, 0:P], rhs=raw[:, 0, 1, :], start=True, stop=True)
         nc.sync.dma_start(out=w_sbuf[:, 0:split], in_=w_dram[:, 0:split])
         nc.vector.memset(w_plane[:].bitcast(I32), 0)
         for q in range(4):
@@ -122,41 +123,50 @@ def tile_stackeddirectionalconv3d_kernel(tc, x, W_words, W_scales, out):
                     in_=col_vals[:, i, b].rearrange("p v j -> p (v j)"),
                 )
 
-        def moving(b, d):
+        def moving(b, d, c0, n):
             if d < 3:
-                lo = (PAD, 0, 2 * PAD)[d]
-                return base_codes[:, b, lo : lo + V], base_scales[:, b, lo : lo + V]
+                lo = (PAD, 0, 2 * PAD)[d] + c0
+                return base_codes[:, b, lo : lo + n], base_scales[:, b, lo : lo + n]
             if d < 5:
-                return row_codes[:, d - 3, b, :], row_scales[:, d - 3, b, :]
-            return col_codes[:, d - 5, b, :], col_scales[:, d - 5, b, :]
+                return row_codes[:, d - 3, b, c0 : c0 + n], row_scales[:, d - 3, b, c0 : c0 + n]
+            return col_codes[:, d - 5, b, c0 : c0 + n], col_scales[:, d - 5, b, c0 : c0 + n]
 
-        def mx_pass(b, o, d):
-            n = OT * d + o
-            codes, scales = moving(b, d)
+        def mx_pass(group, b, o, d, c0, n):
+            w = OT * d + o
+            codes, scales = moving(b, d, c0, n)
             nc.tensor.matmul_mx(
-                out=acc[OT * b + o][:],
-                lhsT=w_words[:, 256 * n : 256 * (n + 1)].bitcast(FP4X4),
-                lhsT_scale=w_plane[:, P * n : P * (n + 1)],
+                out=group,
+                lhsT=w_words[:, 256 * w : 256 * (w + 1)].bitcast(FP4X4),
+                lhsT_scale=w_plane[:, P * w : P * (w + 1)],
                 rhs=codes.bitcast(FP8X4),
                 rhs_scale=scales,
                 start=(d == 0),
                 stop=(d == 6),
             )
 
+        def leave(turn, group, b, o, c0, n):
+            k = OT * b + o
+            if turn % 2 == 0:
+                nc.scalar.copy(out=stage[:, k, c0 : c0 + n], in_=group)
+            else:
+                nc.vector.tensor_copy(out=stage[:, k, c0 : c0 + n], in_=group)
+            nc.sync.dma_start(out=out_view[b, o][:, c0 : c0 + n], in_=stage[:, k, c0 : c0 + n])
+
+        whole = [(b, o) for b in range(B) for o in range(OT)][0 : B * OT - 1]
         for b in range(B):
             quantise_base(b)
             for d in range(3):
-                for o in range(OT):
-                    mx_pass(b, o, d)
+                for k, (bb, o) in enumerate(whole):
+                    if bb == b:
+                        mx_pass(acc[k][:], b, o, d, 0, V)
         for b in range(B):
             shifted(b)
-        for b in range(B):
-            for o in range(OT):
-                for d in range(3, 7):
-                    mx_pass(b, o, d)
-                k = OT * b + o
-                if k % 2 == 0:
-                    nc.scalar.copy(out=stage[:, k, :], in_=acc[k][:])
-                else:
-                    nc.vector.tensor_copy(out=stage[:, k, :], in_=acc[k][:])
-                nc.sync.dma_start(out=out_view[b, o], in_=stage[:, k, :])
+        for k, (b, o) in enumerate(whole):
+            for d in range(3, 7):
+                mx_pass(acc[k][:], b, o, d, 0, V)
+            leave(k, acc[k][:], b, o, 0, V)
+        for g in range(4):
+            part = psum.tile([P, P], F32, name="part%d" % g, tag="acc%d" % g)
+            for d in range(7):
+                mx_pass(part[:], B - 1, OT - 1, d, P * g, P)
+            leave(g, part[:], B - 1, OT - 1, P * g, P)

@@ -42,8 +42,7 @@ def tile_stackeddirectionalconv3d_kernel(tc, x, W_words, W_scales, out):
         w_words = keep.tile([P, 7 * 1024], U8, align_bytes=64)
         w_plane = keep.tile([P, 7 * 512], U8, align_bytes=64)
         stage = keep.tile([P, B * OT, V], F32)
-        acc = [psum.tile([P, V], F32, name="acc%d" % k) for k in range(B * OT - 1)]
-        warm_acc = psum.tile([P, V], F32)
+        acc = [psum.tile([P, V], F32, name="acc%d" % k) for k in range(B * OT)]
 
         x_view = x.rearrange("b (p j) t r c -> b p j (t r c)", j=4)
         out_view = out.rearrange("b (o p) t r c -> b o p (t r c)", p=P)
@@ -52,21 +51,21 @@ def tile_stackeddirectionalconv3d_kernel(tc, x, W_words, W_scales, out):
         split = 3 * 256
 
         nc.sync.dma_start(out=raw[:, 0], in_=x_view[0])
+        nc.sync.dma_start(out=w_sbuf[:, 0:split], in_=w_dram[:, 0:split])
+        nc.sync.dma_start(out=w_sbuf[:, split:], in_=w_dram[:, split:])
+        nc.sync.dma_start(out=raw[:, 1], in_=x_view[1])
+        nc.vector.memset(w_plane[:].bitcast(I32), 0)
+        for q in range(4):
+            nc.scalar.dma_start(
+                out=w_plane[32 * q : 32 * q + 4, :].bitcast(F32),
+                in_=W_scales[0, 4 * q : 4 * q + 4, :].bitcast(F32),
+            )
         warm = keep.tile([P, V], BF16)
         nc.vector.memset(warm[:], 0.0)
         for i in range(WARM_EARLY):
-            nc.tensor.matmul(out=warm_acc[:], lhsT=warm[:, 0:P], rhs=warm[:], start=True, stop=True)
+            nc.tensor.matmul(out=acc[7][:], lhsT=warm[:, 0:P], rhs=warm[:], start=True, stop=True)
         for i in range(WARM_LATE):
-            nc.tensor.matmul(out=warm_acc[:], lhsT=raw[:, 0, 0, 0:P], rhs=raw[:, 0, 1, :], start=True, stop=True)
-        nc.sync.dma_start(out=w_sbuf[:, 0:split], in_=w_dram[:, 0:split])
-        nc.vector.memset(w_plane[:].bitcast(I32), 0)
-        for q in range(4):
-            nc.sync.dma_start(
-                out=w_plane[32 * q : 32 * q + 4, :].bitcast(I32),
-                in_=W_scales[0, 4 * q : 4 * q + 4, :].bitcast(I32),
-            )
-        nc.sync.dma_start(out=raw[:, 1], in_=x_view[1])
-        nc.sync.dma_start(out=w_sbuf[:, split:], in_=w_dram[:, split:])
+            nc.tensor.matmul(out=acc[7][:], lhsT=raw[:, 0, 0, 0:P], rhs=raw[:, 0, 1, :], start=True, stop=True)
 
         nc.vector.memset(
             base_codes[:].bitcast(I32).rearrange("p b (a w) -> p b a w", w=PAD)[:, :, 0:10:9, :], 0
@@ -123,50 +122,40 @@ def tile_stackeddirectionalconv3d_kernel(tc, x, W_words, W_scales, out):
                     in_=col_vals[:, i, b].rearrange("p v j -> p (v j)"),
                 )
 
-        def moving(b, d, c0, n):
+        def moving(b, d):
             if d < 3:
-                lo = (PAD, 0, 2 * PAD)[d] + c0
-                return base_codes[:, b, lo : lo + n], base_scales[:, b, lo : lo + n]
+                lo = (PAD, 0, 2 * PAD)[d]
+                return base_codes[:, b, lo : lo + V], base_scales[:, b, lo : lo + V]
             if d < 5:
-                return row_codes[:, d - 3, b, c0 : c0 + n], row_scales[:, d - 3, b, c0 : c0 + n]
-            return col_codes[:, d - 5, b, c0 : c0 + n], col_scales[:, d - 5, b, c0 : c0 + n]
+                return row_codes[:, d - 3, b, :], row_scales[:, d - 3, b, :]
+            return col_codes[:, d - 5, b, :], col_scales[:, d - 5, b, :]
 
-        def mx_pass(group, b, o, d, c0, n):
-            w = OT * d + o
-            codes, scales = moving(b, d, c0, n)
+        def mx_pass(b, o, d):
+            n = OT * d + o
+            codes, scales = moving(b, d)
             nc.tensor.matmul_mx(
-                out=group,
-                lhsT=w_words[:, 256 * w : 256 * (w + 1)].bitcast(FP4X4),
-                lhsT_scale=w_plane[:, P * w : P * (w + 1)],
+                out=acc[OT * b + o][:],
+                lhsT=w_words[:, 256 * n : 256 * (n + 1)].bitcast(FP4X4),
+                lhsT_scale=w_plane[:, P * n : P * (n + 1)],
                 rhs=codes.bitcast(FP8X4),
                 rhs_scale=scales,
                 start=(d == 0),
                 stop=(d == 6),
             )
 
-        def leave(turn, group, b, o, c0, n):
-            k = OT * b + o
-            if turn % 2 == 0:
-                nc.scalar.copy(out=stage[:, k, c0 : c0 + n], in_=group)
-            else:
-                nc.vector.tensor_copy(out=stage[:, k, c0 : c0 + n], in_=group)
-            nc.sync.dma_start(out=out_view[b, o][:, c0 : c0 + n], in_=stage[:, k, c0 : c0 + n])
-
-        whole = [(b, o) for b in range(B) for o in range(OT)][0 : B * OT - 1]
         for b in range(B):
             quantise_base(b)
-            for d in range(3):
-                for k, (bb, o) in enumerate(whole):
-                    if bb == b:
-                        mx_pass(acc[k][:], b, o, d, 0, V)
-        for b in range(B):
             shifted(b)
-        for k, (b, o) in enumerate(whole):
-            for d in range(3, 7):
-                mx_pass(acc[k][:], b, o, d, 0, V)
-            leave(k, acc[k][:], b, o, 0, V)
-        for g in range(4):
-            part = psum.tile([P, P], F32, name="part%d" % g, tag="acc%d" % g)
-            for d in range(7):
-                mx_pass(part[:], B - 1, OT - 1, d, P * g, P)
-            leave(g, part[:], B - 1, OT - 1, P * g, P)
+        for b in range(B):
+            for d in range(3):
+                for o in range(OT):
+                    mx_pass(b, o, d)
+            for o in range(OT):
+                for d in range(3, 7):
+                    mx_pass(b, o, d)
+                k = OT * b + o
+                if b == B - 1 and o % 2 == 1:
+                    nc.vector.tensor_copy(out=stage[:, k, :], in_=acc[k][:])
+                else:
+                    nc.scalar.copy(out=stage[:, k, :], in_=acc[k][:])
+                nc.sync.dma_start(out=out_view[b, o], in_=stage[:, k, :])

@@ -17,10 +17,9 @@ OT = 4
 PAD = 64
 FLOPS = 2 * B * V * 512 * 7 * 512
 
-V_FIRST = 256
-V_SPLIT = 336
+Q = 128
 WARM_EARLY = 5
-WARM_LATE = 3
+WARM_LATE = 2
 
 
 def tile_stackeddirectionalconv3d_kernel(tc, x, W_words, W_scales, out):
@@ -48,20 +47,23 @@ def tile_stackeddirectionalconv3d_kernel(tc, x, W_words, W_scales, out):
         out_view = out.rearrange("b (o p) t r c -> b o p (t r c)", p=P)
         w_dram = W_words[0].bitcast(I32)
         w_sbuf = w_words[:].bitcast(I32)
-        split = 3 * 256
+
+        def load_w(d0, d1):
+            nc.sync.dma_start(out=w_sbuf[:, 256 * d0 : 256 * d1], in_=w_dram[:, 256 * d0 : 256 * d1])
 
         nc.sync.dma_start(out=raw[:, 0], in_=x_view[0])
-        nc.sync.dma_start(out=w_sbuf[:, 0:split], in_=w_dram[:, 0:split])
-        nc.sync.dma_start(out=w_sbuf[:, split:], in_=w_dram[:, split:])
-        nc.sync.dma_start(out=raw[:, 1], in_=x_view[1])
-        nc.vector.memset(w_plane[:].bitcast(I32), 0)
-        for q in range(4):
-            nc.scalar.dma_start(
-                out=w_plane[32 * q : 32 * q + 4, :].bitcast(F32),
-                in_=W_scales[0, 4 * q : 4 * q + 4, :].bitcast(F32),
-            )
         warm = keep.tile([P, V], BF16)
         nc.vector.memset(warm[:], 0.0)
+        nc.vector.memset(w_plane[:].bitcast(I32), 0)
+        for q in range(4):
+            nc.sync.dma_start(
+                out=w_plane[32 * q : 32 * q + 4, :].bitcast(I32),
+                in_=W_scales[0, 4 * q : 4 * q + 4, :].bitcast(I32),
+            )
+        load_w(0, 1)
+        load_w(1, 3)
+        nc.sync.dma_start(out=raw[:, 1], in_=x_view[1])
+        load_w(3, 7)
         for i in range(WARM_EARLY):
             nc.tensor.matmul(out=acc[7][:], lhsT=warm[:, 0:P], rhs=warm[:], start=True, stop=True)
         for i in range(WARM_LATE):
@@ -90,17 +92,20 @@ def tile_stackeddirectionalconv3d_kernel(tc, x, W_words, W_scales, out):
                 in_=raw[:, b, :, v0:v1].rearrange("p j (c i) -> p c j i", i=4),
             )
 
+        def quantise_quarter(b, q):
+            lo = Q * q
+            nc.vector.quantize_mx(
+                out=base_codes[:, b, PAD + lo : PAD + lo + Q].bitcast(FP8X4),
+                scales=base_scales[:, b, PAD + lo : PAD + lo + Q],
+                in_=grouped[:, b, lo : lo + Q, :].rearrange("p v j -> p (v j)"),
+            )
+
         def quantise_base(b):
-            regroup(nc.vector.tensor_copy, b, 0, V_FIRST)
-            regroup(nc.scalar.copy, b, V_SPLIT, V)
-            regroup(nc.vector.tensor_copy, b, V_FIRST, V_SPLIT)
-            for h in range(2):
-                lo = 256 * h
-                nc.vector.quantize_mx(
-                    out=base_codes[:, b, PAD + lo : PAD + lo + 256].bitcast(FP8X4),
-                    scales=base_scales[:, b, PAD + lo : PAD + lo + 256],
-                    in_=grouped[:, b, lo : lo + 256, :].rearrange("p v j -> p (v j)"),
-                )
+            for q in range(4):
+                regroup(nc.vector.tensor_copy if q < 3 else nc.scalar.copy, b, Q * q, Q * (q + 1))
+                if q > 0:
+                    quantise_quarter(b, q - 1)
+            quantise_quarter(b, 3)
 
         def shifted(b):
             sc = base_codes[:, b, PAD : PAD + V].bitcast(I32).rearrange("p (t w) -> p t w", w=64)
@@ -122,40 +127,48 @@ def tile_stackeddirectionalconv3d_kernel(tc, x, W_words, W_scales, out):
                     in_=col_vals[:, i, b].rearrange("p v j -> p (v j)"),
                 )
 
-        def moving(b, d):
+        def moving(b, d, c0, n):
             if d < 3:
-                lo = (PAD, 0, 2 * PAD)[d]
-                return base_codes[:, b, lo : lo + V], base_scales[:, b, lo : lo + V]
+                lo = (PAD, 0, 2 * PAD)[d] + c0
+                return base_codes[:, b, lo : lo + n], base_scales[:, b, lo : lo + n]
             if d < 5:
-                return row_codes[:, d - 3, b, :], row_scales[:, d - 3, b, :]
-            return col_codes[:, d - 5, b, :], col_scales[:, d - 5, b, :]
+                return row_codes[:, d - 3, b, c0 : c0 + n], row_scales[:, d - 3, b, c0 : c0 + n]
+            return col_codes[:, d - 5, b, c0 : c0 + n], col_scales[:, d - 5, b, c0 : c0 + n]
 
-        def mx_pass(b, o, d):
-            n = OT * d + o
-            codes, scales = moving(b, d)
+        def mx_pass(b, o, d, c0, n):
+            w = OT * d + o
+            codes, scales = moving(b, d, c0, n)
             nc.tensor.matmul_mx(
-                out=acc[OT * b + o][:],
-                lhsT=w_words[:, 256 * n : 256 * (n + 1)].bitcast(FP4X4),
-                lhsT_scale=w_plane[:, P * n : P * (n + 1)],
+                out=acc[OT * b + o][:, c0 : c0 + n],
+                lhsT=w_words[:, 256 * w : 256 * (w + 1)].bitcast(FP4X4),
+                lhsT_scale=w_plane[:, P * w : P * (w + 1)],
                 rhs=codes.bitcast(FP8X4),
                 rhs_scale=scales,
-                start=(d == 0),
+                start=(d == 0 and c0 == 0),
                 stop=(d == 6),
             )
 
         for b in range(B):
             quantise_base(b)
+            if b == 0:
+                for q in range(4):
+                    for o in range(OT):
+                        mx_pass(b, o, 0, Q * q, Q)
+            else:
+                for o in range(OT):
+                    mx_pass(b, o, 0, 0, V)
+            for d in range(1, 3):
+                for o in range(OT):
+                    mx_pass(b, o, d, 0, V)
+        for b in range(B):
             shifted(b)
         for b in range(B):
-            for d in range(3):
-                for o in range(OT):
-                    mx_pass(b, o, d)
             for o in range(OT):
                 for d in range(3, 7):
-                    mx_pass(b, o, d)
+                    mx_pass(b, o, d, 0, V)
                 k = OT * b + o
-                if b == B - 1 and o % 2 == 1:
-                    nc.vector.tensor_copy(out=stage[:, k, :], in_=acc[k][:])
-                else:
+                if k % 2 == 0:
                     nc.scalar.copy(out=stage[:, k, :], in_=acc[k][:])
+                else:
+                    nc.vector.tensor_copy(out=stage[:, k, :], in_=acc[k][:])
                 nc.sync.dma_start(out=out_view[b, o], in_=stage[:, k, :])

@@ -18,8 +18,10 @@ PAD = 64
 FLOPS = 2 * B * V * 512 * 7 * 512
 
 Q = 128
-WARM_EARLY = 5
-WARM_LATE = 2
+H = 256
+DA = 3
+WARM_EARLY = 4
+WARM_LATE = 1
 
 
 def tile_stackeddirectionalconv3d_kernel(tc, x, W_words, W_scales, out):
@@ -29,7 +31,8 @@ def tile_stackeddirectionalconv3d_kernel(tc, x, W_words, W_scales, out):
         psum = ctx.enter_context(tc.psum_pool(name="psum", bufs=1))
         ctx.enter_context(tc.manual_schedule())
 
-        raw = keep.tile([P, B, 4, V], BF16)
+        raw0 = [keep.tile([P, 4, H], BF16, name="raw0h%d" % h) for h in range(2)]
+        raw1 = keep.tile([P, 4, V], BF16)
         grouped = keep.tile([P, B, V, 4], BF16, align_bytes=64)
         base_codes = keep.tile([P, B, V + 2 * PAD], U32, align_bytes=64)
         base_scales = keep.tile([P, B, V + 2 * PAD], U8, align_bytes=64)
@@ -39,7 +42,9 @@ def tile_stackeddirectionalconv3d_kernel(tc, x, W_words, W_scales, out):
         col_codes = keep.tile([P, 2, B, V], U32, align_bytes=64)
         col_scales = keep.tile([P, 2, B, V], U8, align_bytes=64)
         w_words = keep.tile([P, 7 * 1024], U8, align_bytes=64)
-        w_plane = keep.tile([P, 7 * 512], U8, align_bytes=64)
+        plane_a = keep.tile([P, DA * 512], U8, align_bytes=64)
+        plane_b = keep.tile([P, (7 - DA) * 512], U8, align_bytes=64)
+        warm = keep.tile([P, V], BF16)
         stage = keep.tile([P, B * OT, V], F32)
         acc = [psum.tile([P, V], F32, name="acc%d" % k) for k in range(B * OT)]
 
@@ -51,75 +56,89 @@ def tile_stackeddirectionalconv3d_kernel(tc, x, W_words, W_scales, out):
         def load_w(d0, d1):
             nc.sync.dma_start(out=w_sbuf[:, 256 * d0 : 256 * d1], in_=w_dram[:, 256 * d0 : 256 * d1])
 
-        nc.sync.dma_start(out=raw[:, 0], in_=x_view[0])
-        warm = keep.tile([P, V], BF16)
-        nc.vector.memset(warm[:], 0.0)
-        nc.vector.memset(w_plane[:].bitcast(I32), 0)
-        for q in range(4):
-            nc.sync.dma_start(
-                out=w_plane[32 * q : 32 * q + 4, :].bitcast(I32),
-                in_=W_scales[0, 4 * q : 4 * q + 4, :].bitcast(I32),
-            )
+        def load_x0(h):
+            nc.sync.dma_start(out=raw0[h][:], in_=x_view[0][:, :, H * h : H * (h + 1)])
+
+        def load_scales(plane, d0, d1):
+            for g in range(4):
+                nc.sync.dma_start(
+                    out=plane[32 * g : 32 * g + 4, :].bitcast(I32),
+                    in_=W_scales[0, 4 * g : 4 * g + 4, 512 * d0 : 512 * d1].bitcast(I32),
+                )
+
+        nc.gpsimd.memset(warm[:], 0.0)
+        load_x0(0)
         load_w(0, 1)
+        nc.vector.memset(plane_a[:].bitcast(I32), 0)
+        load_scales(plane_a, 0, DA)
+        load_x0(1)
         load_w(1, 3)
-        nc.sync.dma_start(out=raw[:, 1], in_=x_view[1])
-        load_w(3, 7)
+        nc.vector.memset(plane_b[:].bitcast(I32), 0)
+        load_scales(plane_b, DA, 7)
+        load_w(3, 5)
+        nc.sync.dma_start(out=raw1[:], in_=x_view[1])
+        load_w(5, 7)
         for i in range(WARM_EARLY):
             nc.tensor.matmul(out=acc[7][:], lhsT=warm[:, 0:P], rhs=warm[:], start=True, stop=True)
         for i in range(WARM_LATE):
-            nc.tensor.matmul(out=acc[7][:], lhsT=raw[:, 0, 0, 0:P], rhs=raw[:, 0, 1, :], start=True, stop=True)
-
+            nc.tensor.matmul(
+                out=acc[7][:],
+                lhsT=raw0[0][:, 0, 0:P],
+                rhs=raw0[0][:, 0:2, :].rearrange("p j v -> p (j v)"),
+                start=True,
+                stop=True,
+            )
         nc.vector.memset(
             base_codes[:].bitcast(I32).rearrange("p b (a w) -> p b a w", w=PAD)[:, :, 0:10:9, :], 0
         )
         nc.vector.memset(base_scales[:].bitcast(I32), 0)
-        for i in range(2):
-            rc = row_codes[:, i].bitcast(I32).rearrange("p b (t w) -> p (b t) w", w=64)
-            rs = row_scales[:, i].bitcast(I32).rearrange("p b (t w) -> p (b t) w", w=16)
-            cv = col_vals[:, i].rearrange("p b (s c) j -> p (b s) (c j)", c=8)
-            if i == 0:
-                nc.vector.memset(rc[:, :, 0:8], 0)
-                nc.vector.memset(rs[:, :, 0:2], 0)
-                nc.vector.memset(cv[:, :, 0:4], 0.0)
+
+        def row_borders():
+            rc = [row_codes[:, i].bitcast(I32).rearrange("p b (t w) -> p (b t) w", w=64) for i in range(2)]
+            nc.vector.memset(rc[0][:, :, 0:8], 0)
+            nc.vector.memset(rc[1][:, :, 56:64], 0)
+
+        def col_borders():
+            cv = [col_vals[:, i].rearrange("p b (s c) j -> p (b s) (c j)", c=8) for i in range(2)]
+            nc.vector.memset(cv[0][:, :, 0:4], 0.0)
+            nc.vector.memset(cv[1][:, :, 28:32], 0.0)
+
+        def regroup(copy, b, q):
+            if b == 0:
+                src = raw0[q // 2][:, :, Q * (q % 2) : Q * (q % 2 + 1)]
             else:
-                nc.vector.memset(rc[:, :, 56:64], 0)
-                nc.vector.memset(rs[:, :, 14:16], 0)
-                nc.vector.memset(cv[:, :, 28:32], 0.0)
-
-        def regroup(copy, b, v0, v1):
+                src = raw1[:, :, Q * q : Q * (q + 1)]
             copy(
-                out=grouped[:, b, v0:v1, :].rearrange("p (c i) j -> p c j i", i=4),
-                in_=raw[:, b, :, v0:v1].rearrange("p j (c i) -> p c j i", i=4),
+                out=grouped[:, b, Q * q : Q * (q + 1), :].rearrange("p (c i) j -> p c j i", i=4),
+                in_=src.rearrange("p j (c i) -> p c j i", i=4),
             )
 
-        def quantise_quarter(b, q):
-            lo = Q * q
+        def quantise(b, lo, n):
             nc.vector.quantize_mx(
-                out=base_codes[:, b, PAD + lo : PAD + lo + Q].bitcast(FP8X4),
-                scales=base_scales[:, b, PAD + lo : PAD + lo + Q],
-                in_=grouped[:, b, lo : lo + Q, :].rearrange("p v j -> p (v j)"),
+                out=base_codes[:, b, PAD + lo : PAD + lo + n].bitcast(FP8X4),
+                scales=base_scales[:, b, PAD + lo : PAD + lo + n],
+                in_=grouped[:, b, lo : lo + n, :].rearrange("p v j -> p (v j)"),
             )
 
-        def quantise_base(b):
-            for q in range(4):
-                regroup(nc.vector.tensor_copy if q < 3 else nc.scalar.copy, b, Q * q, Q * (q + 1))
-                if q > 0:
-                    quantise_quarter(b, q - 1)
-            quantise_quarter(b, 3)
-
-        def shifted(b):
+        def rows(b):
             sc = base_codes[:, b, PAD : PAD + V].bitcast(I32).rearrange("p (t w) -> p t w", w=64)
-            ss = base_scales[:, b, PAD : PAD + V].bitcast(I32).rearrange("p (t w) -> p t w", w=16)
-            g = grouped[:, b].rearrange("p (s c) j -> p s (c j)", c=8)
             dc = [row_codes[:, i, b, :].bitcast(I32).rearrange("p (t w) -> p t w", w=64) for i in range(2)]
-            ds = [row_scales[:, i, b, :].bitcast(I32).rearrange("p (t w) -> p t w", w=16) for i in range(2)]
-            dv = [col_vals[:, i, b].rearrange("p (s c) j -> p s (c j)", c=8) for i in range(2)]
             nc.vector.tensor_copy(out=dc[0][:, :, 8:64], in_=sc[:, :, 0:56])
-            nc.vector.tensor_copy(out=ds[0][:, :, 2:16], in_=ss[:, :, 0:14])
             nc.vector.tensor_copy(out=dc[1][:, :, 0:56], in_=sc[:, :, 8:64])
-            nc.vector.tensor_copy(out=ds[1][:, :, 0:14], in_=ss[:, :, 2:16])
-            nc.vector.tensor_copy(out=dv[0][:, :, 4:32], in_=g[:, :, 0:28])
-            nc.vector.tensor_copy(out=dv[1][:, :, 0:28], in_=g[:, :, 4:32])
+            nc.vector.tensor_copy(
+                out=row_scales[:, 0, b, :].bitcast(I32), in_=base_scales[:, b, PAD - 8 : PAD - 8 + V].bitcast(I32)
+            )
+            nc.vector.tensor_copy(
+                out=row_scales[:, 1, b, :].bitcast(I32), in_=base_scales[:, b, PAD + 8 : PAD + 8 + V].bitcast(I32)
+            )
+
+        def shift_cols(b):
+            g = grouped[:, b].rearrange("p (s c) j -> p s (c j)", c=8)
+            dv = [col_vals[:, i, b].rearrange("p (s c) j -> p s (c j)", c=8) for i in range(2)]
+            nc.scalar.copy(out=dv[0][:, :, 4:32], in_=g[:, :, 0:28])
+            nc.scalar.copy(out=dv[1][:, :, 0:28], in_=g[:, :, 4:32])
+
+        def quantise_cols(b):
             for i in range(2):
                 nc.vector.quantize_mx(
                     out=col_codes[:, i, b, :].bitcast(FP8X4),
@@ -138,37 +157,61 @@ def tile_stackeddirectionalconv3d_kernel(tc, x, W_words, W_scales, out):
         def mx_pass(b, o, d, c0, n):
             w = OT * d + o
             codes, scales = moving(b, d, c0, n)
+            if d < DA:
+                w_scale = plane_a[:, P * w : P * (w + 1)]
+            else:
+                w_scale = plane_b[:, P * (w - OT * DA) : P * (w - OT * DA + 1)]
             nc.tensor.matmul_mx(
                 out=acc[OT * b + o][:, c0 : c0 + n],
                 lhsT=w_words[:, 256 * w : 256 * (w + 1)].bitcast(FP4X4),
-                lhsT_scale=w_plane[:, P * w : P * (w + 1)],
+                lhsT_scale=w_scale,
                 rhs=codes.bitcast(FP8X4),
                 rhs_scale=scales,
                 start=(d == 0 and c0 == 0),
                 stop=(d == 6),
             )
 
-        for b in range(B):
-            quantise_base(b)
-            if b == 0:
-                for q in range(4):
-                    for o in range(OT):
-                        mx_pass(b, o, 0, Q * q, Q)
-            else:
-                for o in range(OT):
-                    mx_pass(b, o, 0, 0, V)
-            for d in range(1, 3):
-                for o in range(OT):
-                    mx_pass(b, o, d, 0, V)
-        for b in range(B):
-            shifted(b)
-        for b in range(B):
+        def empty(copy, b, o):
+            k = OT * b + o
+            copy(out=stage[:, k, :], in_=acc[k][:])
+            nc.sync.dma_start(out=out_view[b, o], in_=stage[:, k, :])
+
+        for h in range(2):
+            regroup(nc.vector.tensor_copy, 0, 2 * h)
+            regroup(nc.scalar.copy, 0, 2 * h + 1)
+            quantise(0, Q * 2 * h, Q)
+            quantise(0, Q * (2 * h + 1), Q)
+        for q in range(4):
             for o in range(OT):
-                for d in range(3, 7):
-                    mx_pass(b, o, d, 0, V)
-                k = OT * b + o
-                if k % 2 == 0:
-                    nc.scalar.copy(out=stage[:, k, :], in_=acc[k][:])
-                else:
-                    nc.vector.tensor_copy(out=stage[:, k, :], in_=acc[k][:])
-                nc.sync.dma_start(out=out_view[b, o], in_=stage[:, k, :])
+                mx_pass(0, o, 0, Q * q, Q)
+        for d in range(1, 3):
+            for o in range(OT):
+                mx_pass(0, o, d, 0, V)
+        shift_cols(0)
+        row_borders()
+        rows(0)
+        for d in range(3, 5):
+            for o in range(OT):
+                mx_pass(0, o, d, 0, V)
+        col_borders()
+        quantise_cols(0)
+
+        for q in range(4):
+            regroup(nc.vector.tensor_copy if q % 2 == 0 else nc.scalar.copy, 1, q)
+        quantise(1, 0, V)
+        shift_cols(1)
+        rows(1)
+        quantise_cols(1)
+
+        for o in range(OT):
+            for d in range(5, 7):
+                mx_pass(0, o, d, 0, V)
+            empty(nc.scalar.copy if o % 2 == 0 else nc.vector.tensor_copy, 0, o)
+
+        for d in range(3):
+            for o in range(OT):
+                mx_pass(1, o, d, 0, V)
+        for o in range(OT):
+            for d in range(3, 7):
+                mx_pass(1, o, d, 0, V)
+            empty(nc.scalar.copy if o % 2 == 0 else nc.vector.tensor_copy, 1, o)

@@ -68,11 +68,11 @@ def tile_stackeddirectionalconv3d_kernel(tc, x, W_words, W_scales, out):
 
         nc.gpsimd.memset(warm[:], 0.0)
         load_x0(0)
-        load_w(0, 1)
+        load_w(0, 2)
         nc.vector.memset(plane_a[:].bitcast(I32), 0)
         load_scales(plane_a, 0, DA)
         load_x0(1)
-        load_w(1, 3)
+        load_w(2, 3)
         nc.vector.memset(plane_b[:].bitcast(I32), 0)
         load_scales(plane_b, DA, 7)
         load_w(3, 5)
@@ -171,22 +171,23 @@ def tile_stackeddirectionalconv3d_kernel(tc, x, W_words, W_scales, out):
                 stop=(d == 6),
             )
 
-        def empty(copy, b, o):
+        def empty(copy, b, o, pieces=1):
             k = OT * b + o
-            copy(out=stage[:, k, :], in_=acc[k][:])
-            nc.sync.dma_start(out=out_view[b, o], in_=stage[:, k, :])
+            n = V // pieces
+            for c0 in range(0, V, n):
+                copy(out=stage[:, k, c0 : c0 + n], in_=acc[k][:, c0 : c0 + n])
+                nc.sync.dma_start(out=out_view[b, o][:, c0 : c0 + n], in_=stage[:, k, c0 : c0 + n])
 
         for h in range(2):
             regroup(nc.vector.tensor_copy, 0, 2 * h)
             regroup(nc.scalar.copy, 0, 2 * h + 1)
             quantise(0, Q * 2 * h, Q)
             quantise(0, Q * (2 * h + 1), Q)
-        for q in range(4):
+        for d, q in ((0, 0), (0, 1), (1, 0), (1, 1), (0, 2), (1, 2), (0, 3), (1, 3)):
             for o in range(OT):
-                mx_pass(0, o, 0, Q * q, Q)
-        for d in range(1, 3):
-            for o in range(OT):
-                mx_pass(0, o, d, 0, V)
+                mx_pass(0, o, d, Q * q, Q)
+        for o in range(OT):
+            mx_pass(0, o, 2, 0, V)
         shift_cols(0)
         row_borders()
         rows(0)
@@ -214,4 +215,4 @@ def tile_stackeddirectionalconv3d_kernel(tc, x, W_words, W_scales, out):
         for o in range(OT):
             for d in range(3, 7):
                 mx_pass(1, o, d, 0, V)
-            empty(nc.scalar.copy if o % 2 == 0 else nc.vector.tensor_copy, 1, o)
+            empty(nc.scalar.copy if o % 2 == 0 else nc.vector.tensor_copy, 1, o, pieces=(2 if o == OT - 1 else 1))

@@ -154,20 +154,21 @@ def tile_stackeddirectionalconv3d_kernel(tc, x, W_words, W_scales, out):
                 return row_codes[:, d - 3, b, c0 : c0 + n], row_scales[:, d - 3, b, c0 : c0 + n]
             return col_codes[:, d - 5, b, c0 : c0 + n], col_scales[:, d - 5, b, c0 : c0 + n]
 
-        def mx_pass(b, o, d, c0, n):
+        def mx_pass(b, o, d, c0, n, bank=None):
             w = OT * d + o
             codes, scales = moving(b, d, c0, n)
+            target = acc[OT * b + o][:, c0 : c0 + n] if bank is None else bank
             if d < DA:
                 w_scale = plane_a[:, P * w : P * (w + 1)]
             else:
                 w_scale = plane_b[:, P * (w - OT * DA) : P * (w - OT * DA + 1)]
             nc.tensor.matmul_mx(
-                out=acc[OT * b + o][:, c0 : c0 + n],
+                out=target,
                 lhsT=w_words[:, 256 * w : 256 * (w + 1)].bitcast(FP4X4),
                 lhsT_scale=w_scale,
                 rhs=codes.bitcast(FP8X4),
                 rhs_scale=scales,
-                start=(d == 0 and c0 == 0),
+                start=(d == 0 and (c0 == 0 or bank is not None)),
                 stop=(d == 6),
             )
 
@@ -210,9 +211,19 @@ def tile_stackeddirectionalconv3d_kernel(tc, x, W_words, W_scales, out):
             empty(nc.scalar.copy if o % 2 == 0 else nc.vector.tensor_copy, 0, o)
 
         for d in range(3):
-            for o in range(OT):
+            for o in range(OT - 1):
                 mx_pass(1, o, d, 0, V)
-        for o in range(OT):
+        for o in range(OT - 1):
             for d in range(3, 7):
                 mx_pass(1, o, d, 0, V)
-            empty(nc.scalar.copy if o % 2 == 0 else nc.vector.tensor_copy, 1, o, pieces=(2 if o == OT - 1 else 1))
+            empty(nc.scalar.copy if o % 2 == 0 else nc.vector.tensor_copy, 1, o)
+
+        last = OT - 1
+        for q in range(4):
+            for d in range(7):
+                mx_pass(1, last, d, Q * q, Q, bank=acc[q][:, 0:Q])
+            copy = nc.scalar.copy if q % 2 == 0 else nc.vector.tensor_copy
+            copy(out=stage[:, OT + last, Q * q : Q * (q + 1)], in_=acc[q][:, 0:Q])
+            nc.sync.dma_start(
+                out=out_view[1, last][:, Q * q : Q * (q + 1)], in_=stage[:, OT + last, Q * q : Q * (q + 1)]
+            )

@@ -68,16 +68,16 @@ def tile_stackeddirectionalconv3d_kernel(tc, x, W_words, W_scales, out):
 
         nc.gpsimd.memset(warm[:], 0.0)
         load_x0(0)
-        load_w(0, 2)
+        load_w(0, 1)
         nc.vector.memset(plane_a[:].bitcast(I32), 0)
         load_scales(plane_a, 0, DA)
         load_x0(1)
-        load_w(2, 3)
+        load_w(1, 2)
+        load_w(2, 5)
         nc.vector.memset(plane_b[:].bitcast(I32), 0)
         load_scales(plane_b, DA, 7)
-        load_w(3, 5)
-        nc.sync.dma_start(out=raw1[:], in_=x_view[1])
         load_w(5, 7)
+        nc.sync.dma_start(out=raw1[:], in_=x_view[1])
         for i in range(WARM_EARLY):
             nc.tensor.matmul(out=acc[7][:], lhsT=warm[:, 0:P], rhs=warm[:], start=True, stop=True)
         for i in range(WARM_LATE):

@@ -15,6 +15,7 @@ B = 2
 V = 512
 OT = 4
 PAD = 64
+W_START = 128
 FLOPS = 2 * B * V * 512 * 7 * 512
 
 Q = 128
@@ -41,7 +42,8 @@ def tile_stackeddirectionalconv3d_kernel(tc, x, W_words, W_scales, out):
         col_vals = keep.tile([P, 2, B, V, 4], BF16, align_bytes=64)
         col_codes = keep.tile([P, 2, B, V], U32, align_bytes=64)
         col_scales = keep.tile([P, 2, B, V], U8, align_bytes=64)
-        w_words = keep.tile([P, 7 * 1024], U8, align_bytes=64)
+        w_tile = keep.tile([P, W_START + 7 * 1024 + W_START], U8, align_bytes=256)
+        w_words = w_tile[:, W_START : W_START + 7 * 1024]
         plane_a = keep.tile([P, DA * 512], U8, align_bytes=64)
         plane_b = keep.tile([P, (7 - DA) * 512], U8, align_bytes=64)
         warm = keep.tile([P, V], BF16)
@@ -51,7 +53,7 @@ def tile_stackeddirectionalconv3d_kernel(tc, x, W_words, W_scales, out):
         x_view = x.rearrange("b (p j) t r c -> b p j (t r c)", j=4)
         out_view = out.rearrange("b (o p) t r c -> b o p (t r c)", p=P)
         w_dram = W_words[0].bitcast(I32)
-        w_sbuf = w_words[:].bitcast(I32)
+        w_sbuf = w_words.bitcast(I32)
 
         def load_w(d0, d1):
             nc.sync.dma_start(out=w_sbuf[:, 256 * d0 : 256 * d1], in_=w_dram[:, 256 * d0 : 256 * d1])

@@ -46,7 +46,7 @@ def tile_stackeddirectionalconv3d_kernel(tc, x, W_words, W_scales, out):
         w_words = w_tile[:, W_START : W_START + 7 * 1024]
         plane_a = keep.tile([P, DA * 512], U8, align_bytes=64)
         plane_b = keep.tile([P, (7 - DA) * 512], U8, align_bytes=64)
-        warm = keep.tile([P, V], BF16)
+        warm = keep.tile([P, P], F32)
         stage = keep.tile([P, B * OT, V], F32)
         acc = [psum.tile([P, V], F32, name="acc%d" % k) for k in range(B * OT)]
 
@@ -68,7 +68,7 @@ def tile_stackeddirectionalconv3d_kernel(tc, x, W_words, W_scales, out):
                     in_=W_scales[0, 4 * g : 4 * g + 4, 512 * d0 : 512 * d1].bitcast(I32),
                 )
 
-        nc.gpsimd.memset(warm[:], 0.0)
+        nc.vector.memset(warm[:], 0.0)
         load_x0(0)
         load_w(0, 1)
         nc.vector.memset(plane_a[:].bitcast(I32), 0)
@@ -81,7 +81,7 @@ def tile_stackeddirectionalconv3d_kernel(tc, x, W_words, W_scales, out):
         load_w(5, 7)
         nc.sync.dma_start(out=raw1[:], in_=x_view[1])
         for i in range(WARM_EARLY):
-            nc.tensor.matmul(out=acc[7][:], lhsT=warm[:, 0:P], rhs=warm[:], start=True, stop=True)
+            nc.tensor.matmul(out=acc[7][:, 0:P], lhsT=warm[:], rhs=warm[:], start=True, stop=True)
         for i in range(WARM_LATE):
             nc.tensor.matmul(
                 out=acc[7][:],

from contextlib import ExitStack

import concourse.mybir as mybir

BF16 = mybir.dt.bfloat16
F32 = mybir.dt.float32
I32 = mybir.dt.int32
U32 = mybir.dt.uint32
U8 = mybir.dt.uint8
FP8X4 = mybir.dt.float8_e4m3fn_x4
FP4X4 = mybir.dt.float4_e2m1fn_x4

P = 128
B = 2
V = 512
OT = 4
PAD = 64
W_START = 128
FLOPS = 2 * B * V * 512 * 7 * 512

Q = 128
H = 256
DA = 3
WARM_EARLY = 4
WARM_LATE = 1


def tile_stackeddirectionalconv3d_kernel(tc, x, W_words, W_scales, out):
    nc = tc.nc
    with ExitStack() as ctx:
        keep = ctx.enter_context(tc.tile_pool(name="keep", bufs=1))
        psum = ctx.enter_context(tc.psum_pool(name="psum", bufs=1))
        ctx.enter_context(tc.manual_schedule())

        raw0 = [keep.tile([P, 4, H], BF16, name="raw0h%d" % h) for h in range(2)]
        raw1 = keep.tile([P, 4, V], BF16)
        grouped = keep.tile([P, B, V, 4], BF16, align_bytes=64)
        base_codes = keep.tile([P, B, V + 2 * PAD], U32, align_bytes=64)
        base_scales = keep.tile([P, B, V + 2 * PAD], U8, align_bytes=64)
        row_codes = keep.tile([P, 2, B, V], U32, align_bytes=64)
        row_scales = keep.tile([P, 2, B, V], U8, align_bytes=64)
        col_vals = keep.tile([P, 2, B, V, 4], BF16, align_bytes=64)
        col_codes = keep.tile([P, 2, B, V], U32, align_bytes=64)
        col_scales = keep.tile([P, 2, B, V], U8, align_bytes=64)
        w_tile = keep.tile([P, W_START + 7 * 1024 + W_START], U8, align_bytes=256)
        w_words = w_tile[:, W_START : W_START + 7 * 1024]
        plane_a = keep.tile([P, DA * 512], U8, align_bytes=64)
        plane_b = keep.tile([P, (7 - DA) * 512], U8, align_bytes=64)
        warm = keep.tile([P, P], F32)
        stage = keep.tile([P, B * OT, V], F32)
        acc = [psum.tile([P, V], F32, name="acc%d" % k) for k in range(B * OT)]

        x_view = x.rearrange("b (p j) t r c -> b p j (t r c)", j=4)
        out_view = out.rearrange("b (o p) t r c -> b o p (t r c)", p=P)
        w_dram = W_words[0].bitcast(I32)
        w_sbuf = w_words.bitcast(I32)

        def load_w(d0, d1):
            nc.sync.dma_start(out=w_sbuf[:, 256 * d0 : 256 * d1], in_=w_dram[:, 256 * d0 : 256 * d1])

        def load_x0(h):
            nc.sync.dma_start(out=raw0[h][:], in_=x_view[0][:, :, H * h : H * (h + 1)])

        def load_scales(plane, d0, d1):
            for g in range(4):
                nc.sync.dma_start(
                    out=plane[32 * g : 32 * g + 4, :].bitcast(I32),
                    in_=W_scales[0, 4 * g : 4 * g + 4, 512 * d0 : 512 * d1].bitcast(I32),
                )

        nc.vector.memset(warm[:], 0.0)
        load_x0(0)
        load_w(0, 1)
        nc.vector.memset(plane_a[:].bitcast(I32), 0)
        load_scales(plane_a, 0, DA)
        load_x0(1)
        load_w(1, 2)
        load_w(2, 5)
        nc.vector.memset(plane_b[:].bitcast(I32), 0)
        load_scales(plane_b, DA, 7)
        load_w(5, 7)
        nc.sync.dma_start(out=raw1[:], in_=x_view[1])
        for i in range(WARM_EARLY):
            nc.tensor.matmul(out=acc[7][:, 0:P], lhsT=warm[:], rhs=warm[:], start=True, stop=True)
        for i in range(WARM_LATE):
            nc.tensor.matmul(
                out=acc[7][:],
                lhsT=raw0[0][:, 0, 0:P],
                rhs=raw0[0][:, 0:2, :].rearrange("p j v -> p (j v)"),
                start=True,
                stop=True,
            )
        nc.vector.memset(
            base_codes[:].bitcast(I32).rearrange("p b (a w) -> p b a w", w=PAD)[:, :, 0:10:9, :], 0
        )
        nc.vector.memset(base_scales[:].bitcast(I32), 0)

        def row_borders():
            rc = [row_codes[:, i].bitcast(I32).rearrange("p b (t w) -> p (b t) w", w=64) for i in range(2)]
            nc.vector.memset(rc[0][:, :, 0:8], 0)
            nc.vector.memset(rc[1][:, :, 56:64], 0)

        def col_borders():
            cv = [col_vals[:, i].rearrange("p b (s c) j -> p (b s) (c j)", c=8) for i in range(2)]
            nc.vector.memset(cv[0][:, :, 0:4], 0.0)
            nc.vector.memset(cv[1][:, :, 28:32], 0.0)

        def regroup(copy, b, q):
            if b == 0:
                src = raw0[q // 2][:, :, Q * (q % 2) : Q * (q % 2 + 1)]
            else:
                src = raw1[:, :, Q * q : Q * (q + 1)]
            copy(
                out=grouped[:, b, Q * q : Q * (q + 1), :].rearrange("p (c i) j -> p c j i", i=4),
                in_=src.rearrange("p j (c i) -> p c j i", i=4),
            )

        def quantise(b, lo, n):
            nc.vector.quantize_mx(
                out=base_codes[:, b, PAD + lo : PAD + lo + n].bitcast(FP8X4),
                scales=base_scales[:, b, PAD + lo : PAD + lo + n],
                in_=grouped[:, b, lo : lo + n, :].rearrange("p v j -> p (v j)"),
            )

        def rows(b):
            sc = base_codes[:, b, PAD : PAD + V].bitcast(I32).rearrange("p (t w) -> p t w", w=64)
            dc = [row_codes[:, i, b, :].bitcast(I32).rearrange("p (t w) -> p t w", w=64) for i in range(2)]
            nc.vector.tensor_copy(out=dc[0][:, :, 8:64], in_=sc[:, :, 0:56])
            nc.vector.tensor_copy(out=dc[1][:, :, 0:56], in_=sc[:, :, 8:64])
            nc.vector.tensor_copy(
                out=row_scales[:, 0, b, :].bitcast(I32), in_=base_scales[:, b, PAD - 8 : PAD - 8 + V].bitcast(I32)
            )
            nc.vector.tensor_copy(
                out=row_scales[:, 1, b, :].bitcast(I32), in_=base_scales[:, b, PAD + 8 : PAD + 8 + V].bitcast(I32)
            )

        def shift_cols(b):
            g = grouped[:, b].rearrange("p (s c) j -> p s (c j)", c=8)
            dv = [col_vals[:, i, b].rearrange("p (s c) j -> p s (c j)", c=8) for i in range(2)]
            nc.scalar.copy(out=dv[0][:, :, 4:32], in_=g[:, :, 0:28])
            nc.scalar.copy(out=dv[1][:, :, 0:28], in_=g[:, :, 4:32])

        def quantise_cols(b):
            for i in range(2):
                nc.vector.quantize_mx(
                    out=col_codes[:, i, b, :].bitcast(FP8X4),
                    scales=col_scales[:, i, b, :],
                    in_=col_vals[:, i, b].rearrange("p v j -> p (v j)"),
                )

        def moving(b, d, c0, n):
            if d < 3:
                lo = (PAD, 0, 2 * PAD)[d] + c0
                return base_codes[:, b, lo : lo + n], base_scales[:, b, lo : lo + n]
            if d < 5:
                return row_codes[:, d - 3, b, c0 : c0 + n], row_scales[:, d - 3, b, c0 : c0 + n]
            return col_codes[:, d - 5, b, c0 : c0 + n], col_scales[:, d - 5, b, c0 : c0 + n]

        def mx_pass(b, o, d, c0, n, bank=None):
            w = OT * d + o
            codes, scales = moving(b, d, c0, n)
            target = acc[OT * b + o][:, c0 : c0 + n] if bank is None else bank
            if d < DA:
                w_scale = plane_a[:, P * w : P * (w + 1)]
            else:
                w_scale = plane_b[:, P * (w - OT * DA) : P * (w - OT * DA + 1)]
            nc.tensor.matmul_mx(
                out=target,
                lhsT=w_words[:, 256 * w : 256 * (w + 1)].bitcast(FP4X4),
                lhsT_scale=w_scale,
                rhs=codes.bitcast(FP8X4),
                rhs_scale=scales,
                start=(d == 0 and (c0 == 0 or bank is not None)),
                stop=(d == 6),
            )

        def empty(copy, b, o, pieces=1):
            k = OT * b + o
            n = V // pieces
            for c0 in range(0, V, n):
                copy(out=stage[:, k, c0 : c0 + n], in_=acc[k][:, c0 : c0 + n])
                nc.sync.dma_start(out=out_view[b, o][:, c0 : c0 + n], in_=stage[:, k, c0 : c0 + n])

        for h in range(2):
            regroup(nc.vector.tensor_copy, 0, 2 * h)
            regroup(nc.scalar.copy, 0, 2 * h + 1)
            quantise(0, Q * 2 * h, Q)
            quantise(0, Q * (2 * h + 1), Q)
        for d, q in ((0, 0), (0, 1), (1, 0), (1, 1), (0, 2), (1, 2), (0, 3), (1, 3)):
            for o in range(OT):
                mx_pass(0, o, d, Q * q, Q)
        for o in range(OT):
            mx_pass(0, o, 2, 0, V)
        shift_cols(0)
        row_borders()
        rows(0)
        for d in range(3, 5):
            for o in range(OT):
                mx_pass(0, o, d, 0, V)
        col_borders()
        quantise_cols(0)

        for q in range(4):
            regroup(nc.vector.tensor_copy if q % 2 == 0 else nc.scalar.copy, 1, q)
        quantise(1, 0, V)
        shift_cols(1)
        rows(1)
        quantise_cols(1)

        for o in range(OT):
            for d in range(5, 7):
                mx_pass(0, o, d, 0, V)
            empty(nc.scalar.copy if o % 2 == 0 else nc.vector.tensor_copy, 0, o)

        for d in range(3):
            for o in range(OT - 1):
                mx_pass(1, o, d, 0, V)
        for o in range(OT - 1):
            for d in range(3, 7):
                mx_pass(1, o, d, 0, V)
            empty(nc.scalar.copy if o % 2 == 0 else nc.vector.tensor_copy, 1, o)

        last = OT - 1
        for q in range(4):
            for d in range(7):
                mx_pass(1, last, d, Q * q, Q, bank=acc[q][:, 0:Q])
            copy = nc.scalar.copy if q % 2 == 0 else nc.vector.tensor_copy
            copy(out=stage[:, OT + last, Q * q : Q * (q + 1)], in_=acc[q][:, 0:Q])
            nc.sync.dma_start(
                out=out_view[1, last][:, Q * q : Q * (q + 1)], in_=stage[:, OT + last, Q * q : Q * (q + 1)]
            )
